import numpy as np
import ml_dtypes


def mxq(x, axis, fmt="e4m3"):
    dtype, down = {"e4m3": (ml_dtypes.float8_e4m3fn, 7), "e5m2": (ml_dtypes.float8_e5m2, 14)}[fmt]
    v = np.moveaxis(np.asarray(x, np.float32).astype(ml_dtypes.bfloat16).astype(np.float64), axis, -1)
    blocks = v.reshape(v.shape[:-1] + (-1, 32))
    amax = np.abs(blocks).max(-1, keepdims=True)
    byte = np.maximum(np.where(amax > 0, np.frexp(amax)[1] - 1 + 127, 0) - down, 1)
    scale = np.exp2(byte - 127.0)
    codes = (blocks / scale).astype(np.float32).astype(dtype).astype(np.float64)
    return np.moveaxis((codes * scale).reshape(v.shape), -1, axis)


WIDE = False


def mx_kscale(k):
    if not WIDE:
        return np.ones(k)
    levels = np.array([10, -10, 5, -5, 0])
    a = np.random.permutation(np.resize(levels, k // 512 * 4)).reshape(k // 512, 4)
    idx = np.arange(k)
    return np.exp2(a[idx // 512, idx % 128 // 32])


BF16 = ml_dtypes.bfloat16


def bf(x):
    return np.asarray(x, np.float32).astype(BF16)


def f64(x):
    return np.asarray(x).astype(np.float64)


B, L, F, A = 128, 12, 512, 384


def setup_inputs():
    s = mx_kscale(L * F).reshape(L, F)
    thresh = 1.0 / (A * L) ** 0.5
    inp = {"x": bf(np.random.standard_normal((B, L, F)) * s)}
    for i in range(L):
        inp[f"W_{i}"] = bf(np.random.uniform(-thresh, thresh, (i + 1, F, A)) / s[: i + 1, :, None])
    return inp


def reference(x, W_0, W_1, W_2, W_3, W_4, W_5, W_6, W_7, W_8, W_9, W_10, W_11):
    Ws = [W_0, W_1, W_2, W_3, W_4, W_5, W_6, W_7, W_8, W_9, W_10, W_11]
    xq = mxq(f64(x).reshape(B, L * F), 1, "e4m3")
    preds = [
        (xq[:, : (i + 1) * F] @ mxq(f64(Ws[i]).reshape((i + 1) * F, A), 0, "e4m3"))
        for i in range(L)
    ]
    return np.stack(preds, axis=1)

@@ -1,0 +1,165 @@
+from contextlib import ExitStack
+
+import concourse.mybir as mybir
+from concourse.masks import make_identity
+
+BF16 = mybir.dt.bfloat16
+F32 = mybir.dt.float32
+U32 = mybir.dt.uint32
+U8 = mybir.dt.uint8
+FP8X4 = mybir.dt.float8_e4m3fn_x4
+
+P = 128
+PACK = 4
+B = 128
+LAYERS = 12
+F = P * PACK
+A = 384
+
+COLUMN_GROUPS = ((0, 256), (256, 384))
+
+VECTOR_COLS = 192
+
+LOAD_LAYERS = 2
+RAW_BUFS = 12
+
+QUANTISE_LAG = 1
+EVACUATE_LAG = 3
+STORE_LAG = 4
+
+FLOPS = 2 * B * F * A * (LAYERS * (LAYERS + 1) // 2)
+
+
+def runs_of_four(view, order):
+    return view.rearrange(order + " -> p c t i", i=4)
+
+
+def tile_decoder_pa_kernel(
+    tc, x, W_0, W_1, W_2, W_3, W_4, W_5, W_6, W_7, W_8, W_9, W_10, W_11, out
+):
+    nc = tc.nc
+    weights = [W_0, W_1, W_2, W_3, W_4, W_5, W_6, W_7, W_8, W_9, W_10, W_11]
+
+    with ExitStack() as ctx:
+        keep = ctx.enter_context(tc.tile_pool(name="keep", bufs=1))
+        raw_pool = ctx.enter_context(tc.tile_pool(name="raw", bufs=RAW_BUFS))
+        grouped_pool = ctx.enter_context(tc.tile_pool(name="grouped", bufs=4))
+        codes_pool = ctx.enter_context(tc.tile_pool(name="codes", bufs=4))
+        result_pool = ctx.enter_context(tc.tile_pool(name="result", bufs=3))
+        turned_pool = ctx.enter_context(tc.psum_pool(name="turned", bufs=2))
+        acc_pool = ctx.enter_context(tc.psum_pool(name="acc", bufs=3))
+
+        x_rows = keep.tile([B, LAYERS * F], BF16)
+        nc.sync.dma_start(out=x_rows[:], in_=x.rearrange("b l f -> b (l f)"))
+
+        outputs = list(reversed(range(LAYERS)))
+        layers = [(i, l) for i in outputs for l in range(i + 1)]
+        loads = [
+            (i, l0, min(LOAD_LAYERS, i + 1 - l0))
+            for i in outputs
+            for l0 in range(0, i + 1, LOAD_LAYERS)
+        ]
+        load_that_starts_at = dict(((i, l0), c) for c, (i, l0, count) in enumerate(loads))
+        raw_of = {}
+
+        def load(c):
+            i, l0, count = loads[c]
+            raw = raw_pool.tile([P, LOAD_LAYERS, PACK, A], BF16)
+            nc.sync.dma_start(
+                out=raw[:, :count],
+                in_=weights[i][l0 : l0 + count].rearrange("l (p t) a -> p l t a", t=PACK),
+            )
+            for y in range(count):
+                raw_of[(i, l0 + y)] = raw[:, y]
+
+        for c in range(RAW_BUFS - 1):
+            load(c)
+
+        identity = keep.tile([P, P], F32)
+        make_identity(nc, identity[:])
+        x_words = x_rows[:].bitcast(F32).rearrange("b (l p u) -> b l u p", l=LAYERS, u=2)
+        x_grouped = keep.tile([P, LAYERS * B * PACK], BF16, align_bytes=64)
+        x_grouped_words = x_grouped[:].bitcast(F32).rearrange("p (l b u) -> p l b u", l=LAYERS, u=2)
+        x_codes = keep.tile([P, LAYERS * B], U32, align_bytes=64)
+        x_scales = keep.tile([P, LAYERS * B], U8, align_bytes=64)
+        for l0 in range(0, LAYERS, 2):
+            turned = turned_pool.tile([P, 2, 2, B], F32)
+            for y in range(2):
+                for u in range(2):
+                    nc.tensor.transpose(turned[:, y, u, :], x_words[:, l0 + y, u, :], identity[:])
+            nc.scalar.copy(
+                out=x_grouped_words[:, l0 : l0 + 2],
+                in_=turned[:].rearrange("p y u b -> p y b u"),
+            )
+            nc.vector.quantize_mx(
+                out=x_codes[:, l0 * B : (l0 + 2) * B].bitcast(FP8X4),
+                scales=x_scales[:, l0 * B : (l0 + 2) * B],
+                in_=x_grouped[:, l0 * B * PACK : (l0 + 2) * B * PACK],
+            )
+
+        grouped_of = {}
+        acc_of = {}
+        result_of = {}
+
+        def regroup(i, l):
+            raw = raw_of[(i, l)]
+            grouped = grouped_pool.tile([P, A, PACK], BF16, align_bytes=64)
+            nc.vector.tensor_copy(
+                out=runs_of_four(grouped[:, :VECTOR_COLS, :], "p (c i) t"),
+                in_=runs_of_four(raw[:, :, :VECTOR_COLS], "p t (c i)"),
+            )
+            nc.scalar.copy(
+                out=runs_of_four(grouped[:, VECTOR_COLS:, :], "p (c i) t"),
+                in_=runs_of_four(raw[:, :, VECTOR_COLS:], "p t (c i)"),
+            )
+            grouped_of[(i, l)] = grouped
+
+        def quantise_and_multiply(i, l):
+            values = grouped_of[(i, l)][:].rearrange("p a t -> p (a t)")
+            codes = codes_pool.tile([P, A], U32, align_bytes=64)
+            scales = codes_pool.tile([P, A], U8, align_bytes=64)
+            for first, end in COLUMN_GROUPS:
+                nc.vector.quantize_mx(
+                    out=codes[:, first:end].bitcast(FP8X4),
+                    scales=scales[:, first:end],
+                    in_=values[:, first * PACK : end * PACK],
+                )
+            for first, end in COLUMN_GROUPS:
+                if l == 0:
+                    acc = acc_pool.tile([B, end - first], F32, tag="acc%d" % first)
+                    acc_of[(i, first)] = acc
+                nc.tensor.matmul_mx(
+                    out=acc_of[(i, first)][:],
+                    lhsT=x_codes[:, l * B : (l + 1) * B].bitcast(FP8X4),
+                    lhsT_scale=x_scales[:, l * B : (l + 1) * B],
+                    rhs=codes[:, first:end].bitcast(FP8X4),
+                    rhs_scale=scales[:, first:end],
+                    start=(l == 0),
+                    stop=(l == i),
+                )
+
+        def evacuate(i):
+            result = result_pool.tile([B, A], F32)
+            for first, end in COLUMN_GROUPS:
+                nc.scalar.copy(out=result[:, first:end], in_=acc_of[(i, first)][:])
+            result_of[i] = result
+
+        def store(i):
+            nc.sync.dma_start(out=out[:, i, :], in_=result_of[i][:])
+
+        for n in range(len(layers) + STORE_LAG):
+            if n < len(layers):
+                c = load_that_starts_at.get(layers[n])
+                if c is not None and c + RAW_BUFS - 1 < len(loads):
+                    load(c + RAW_BUFS - 1)
+                regroup(*layers[n])
+            if 0 <= n - QUANTISE_LAG < len(layers):
+                quantise_and_multiply(*layers[n - QUANTISE_LAG])
+            if 0 <= n - EVACUATE_LAG < len(layers):
+                i, l = layers[n - EVACUATE_LAG]
+                if l == i:
+                    evacuate(i)
+            if 0 <= n - STORE_LAG < len(layers):
+                i, l = layers[n - STORE_LAG]
+                if l == i:
+                    store(i)

@@ -17,15 +17,21 @@ F = P * PACK
 A = 384
 
 COLUMN_GROUPS = ((0, 256), (256, 384))
+QUANTISE_GROUPS = ((0, 512), (512, 768))
 
-VECTOR_COLS = 192
+SHARED_VECTOR_COLS = 256
 
-LOAD_LAYERS = 2
-RAW_BUFS = 12
+FIRST_LOADS = (1, 1, 2, 2, 2)
+LOAD_LAYERS = 4
+RAW_BUFS = 9
+X_PARTS = 3
+X_LAYERS = LAYERS // X_PARTS
+X_AFTER = 2
 
 QUANTISE_LAG = 1
-EVACUATE_LAG = 3
-STORE_LAG = 4
+MULTIPLY_LAG = 2
+EVACUATE_LAG = 4
+STORE_LAG = 5
 
 FLOPS = 2 * B * F * A * (LAYERS * (LAYERS + 1) // 2)
 
@@ -43,22 +49,24 @@ def tile_decoder_pa_kernel(
     with ExitStack() as ctx:
         keep = ctx.enter_context(tc.tile_pool(name="keep", bufs=1))
         raw_pool = ctx.enter_context(tc.tile_pool(name="raw", bufs=RAW_BUFS))
-        grouped_pool = ctx.enter_context(tc.tile_pool(name="grouped", bufs=4))
-        codes_pool = ctx.enter_context(tc.tile_pool(name="codes", bufs=4))
+        grouped_pool = ctx.enter_context(tc.tile_pool(name="grouped", bufs=6))
+        codes_pool = ctx.enter_context(tc.tile_pool(name="codes", bufs=5))
         result_pool = ctx.enter_context(tc.tile_pool(name="result", bufs=3))
         turned_pool = ctx.enter_context(tc.psum_pool(name="turned", bufs=2))
         acc_pool = ctx.enter_context(tc.psum_pool(name="acc", bufs=3))
 
-        x_rows = keep.tile([B, LAYERS * F], BF16)
-        nc.sync.dma_start(out=x_rows[:], in_=x.rearrange("b l f -> b (l f)"))
-
         outputs = list(reversed(range(LAYERS)))
         layers = [(i, l) for i in outputs for l in range(i + 1)]
-        loads = [
-            (i, l0, min(LOAD_LAYERS, i + 1 - l0))
-            for i in outputs
-            for l0 in range(0, i + 1, LOAD_LAYERS)
-        ]
+        pairs = [layers[n : n + 2] for n in range(0, len(layers), 2)]
+
+        loads = []
+        for i in outputs:
+            l0 = 0
+            while l0 <= i:
+                count = FIRST_LOADS[len(loads)] if len(loads) < len(FIRST_LOADS) else LOAD_LAYERS
+                count = min(count, i + 1 - l0)
+                loads.append((i, l0, count))
+                l0 += count
         load_that_starts_at = dict(((i, l0), c) for c, (i, l0, count) in enumerate(loads))
         raw_of = {}
 
@@ -72,71 +80,98 @@ def tile_decoder_pa_kernel(
             for y in range(count):
                 raw_of[(i, l0 + y)] = raw[:, y]
 
+        x_rows = keep.tile([B, LAYERS, F], BF16)
+
+        def load_x(part):
+            part_layers = slice(part * X_LAYERS, (part + 1) * X_LAYERS)
+            nc.sync.dma_start(out=x_rows[:, part_layers, :], in_=x[:, part_layers, :])
+
         for c in range(RAW_BUFS - 1):
             load(c)
+            if 0 <= c - X_AFTER < X_PARTS:
+                load_x(c - X_AFTER)
 
         identity = keep.tile([P, P], F32)
         make_identity(nc, identity[:])
-        x_words = x_rows[:].bitcast(F32).rearrange("b (l p u) -> b l u p", l=LAYERS, u=2)
+        x_words = x_rows[:].rearrange("b l f -> b (l f)").bitcast(F32)
+        x_words = x_words.rearrange("b (l p u) -> b l u p", l=LAYERS, u=2)
         x_grouped = keep.tile([P, LAYERS * B * PACK], BF16, align_bytes=64)
         x_grouped_words = x_grouped[:].bitcast(F32).rearrange("p (l b u) -> p l b u", l=LAYERS, u=2)
         x_codes = keep.tile([P, LAYERS * B], U32, align_bytes=64)
         x_scales = keep.tile([P, LAYERS * B], U8, align_bytes=64)
-        for l0 in range(0, LAYERS, 2):
-            turned = turned_pool.tile([P, 2, 2, B], F32)
-            for y in range(2):
-                for u in range(2):
-                    nc.tensor.transpose(turned[:, y, u, :], x_words[:, l0 + y, u, :], identity[:])
-            nc.scalar.copy(
-                out=x_grouped_words[:, l0 : l0 + 2],
-                in_=turned[:].rearrange("p y u b -> p y b u"),
-            )
+
+        def turn_x(part):
+            first = part * X_LAYERS
+            for l0 in range(first, first + X_LAYERS, 2):
+                turned = turned_pool.tile([P, 2, 2, B], F32)
+                for y in range(2):
+                    for u in range(2):
+                        nc.tensor.transpose(turned[:, y, u, :], x_words[:, l0 + y, u, :], identity[:])
+                nc.scalar.copy(
+                    out=x_grouped_words[:, l0 : l0 + 2],
+                    in_=turned[:].rearrange("p y u b -> p y b u"),
+                )
+
+        def quantise_x(part):
+            first = part * X_LAYERS
+            columns = slice(first * B, (first + X_LAYERS) * B)
             nc.vector.quantize_mx(
-                out=x_codes[:, l0 * B : (l0 + 2) * B].bitcast(FP8X4),
-                scales=x_scales[:, l0 * B : (l0 + 2) * B],
-                in_=x_grouped[:, l0 * B * PACK : (l0 + 2) * B * PACK],
+                out=x_codes[:, columns].bitcast(FP8X4),
+                scales=x_scales[:, columns],
+                in_=x_grouped[:, first * B * PACK : (first + X_LAYERS) * B * PACK],
             )
 
         grouped_of = {}
         acc_of = {}
         result_of = {}
 
-        def regroup(i, l):
-            raw = raw_of[(i, l)]
-            grouped = grouped_pool.tile([P, A, PACK], BF16, align_bytes=64)
-            nc.vector.tensor_copy(
-                out=runs_of_four(grouped[:, :VECTOR_COLS, :], "p (c i) t"),
-                in_=runs_of_four(raw[:, :, :VECTOR_COLS], "p t (c i)"),
-            )
-            nc.scalar.copy(
-                out=runs_of_four(grouped[:, VECTOR_COLS:, :], "p (c i) t"),
-                in_=runs_of_four(raw[:, :, VECTOR_COLS:], "p t (c i)"),
-            )
-            grouped_of[(i, l)] = grouped
+        def regroup(n):
+            grouped = grouped_pool.tile([P, 2 * A, PACK], BF16, align_bytes=64)
+            grouped_of[n] = grouped
+            for y, layer in enumerate(pairs[n]):
+                raw = raw_of[layer]
+                vector_cols = SHARED_VECTOR_COLS if n in (0, len(pairs) - 1) else (1 - y) * A
+                if vector_cols > 0:
+                    nc.vector.tensor_copy(
+                        out=runs_of_four(grouped[:, y * A : y * A + vector_cols, :], "p (c i) t"),
+                        in_=runs_of_four(raw[:, :, :vector_cols], "p t (c i)"),
+                    )
+                if vector_cols < A:
+                    nc.scalar.copy(
+                        out=runs_of_four(grouped[:, y * A + vector_cols : (y + 1) * A, :], "p (c i) t"),
+                        in_=runs_of_four(raw[:, :, vector_cols:], "p t (c i)"),
+                    )
 
-        def quantise_and_multiply(i, l):
-            values = grouped_of[(i, l)][:].rearrange("p a t -> p (a t)")
-            codes = codes_pool.tile([P, A], U32, align_bytes=64)
-            scales = codes_pool.tile([P, A], U8, align_bytes=64)
-            for first, end in COLUMN_GROUPS:
+        codes_of = {}
+
+        def quantise(n):
+            values = grouped_of[n][:].rearrange("p a t -> p (a t)")
+            codes = codes_pool.tile([P, 2 * A], U32, align_bytes=64)
+            scales = codes_pool.tile([P, 2 * A], U8, align_bytes=64)
+            for first, end in QUANTISE_GROUPS:
                 nc.vector.quantize_mx(
                     out=codes[:, first:end].bitcast(FP8X4),
                     scales=scales[:, first:end],
                     in_=values[:, first * PACK : end * PACK],
                 )
-            for first, end in COLUMN_GROUPS:
-                if l == 0:
-                    acc = acc_pool.tile([B, end - first], F32, tag="acc%d" % first)
-                    acc_of[(i, first)] = acc
-                nc.tensor.matmul_mx(
-                    out=acc_of[(i, first)][:],
-                    lhsT=x_codes[:, l * B : (l + 1) * B].bitcast(FP8X4),
-                    lhsT_scale=x_scales[:, l * B : (l + 1) * B],
-                    rhs=codes[:, first:end].bitcast(FP8X4),
-                    rhs_scale=scales[:, first:end],
-                    start=(l == 0),
-                    stop=(l == i),
-                )
+            codes_of[n] = (codes, scales)
+
+        def multiply(n):
+            codes, scales = codes_of[n]
+            for y, (i, l) in enumerate(pairs[n]):
+                for first, end in COLUMN_GROUPS:
+                    if l == 0:
+                        acc = acc_pool.tile([B, end - first], F32, tag="acc%d" % first)
+                        acc_of[(i, first)] = acc
+                    nc.tensor.matmul_mx(
+                        out=acc_of[(i, first)][:],
+                        lhsT=x_codes[:, l * B : (l + 1) * B].bitcast(FP8X4),
+                        lhsT_scale=x_scales[:, l * B : (l + 1) * B],
+                        rhs=codes[:, y * A + first : y * A + end].bitcast(FP8X4),
+                        rhs_scale=scales[:, y * A + first : y * A + end],
+                        start=(l == 0),
+                        stop=(l == i),
+                    )
 
         def evacuate(i):
             result = result_pool.tile([B, A], F32)
@@ -147,19 +182,27 @@ def tile_decoder_pa_kernel(
         def store(i):
             nc.sync.dma_start(out=out[:, i, :], in_=result_of[i][:])
 
-        for n in range(len(layers) + STORE_LAG):
-            if n < len(layers):
-                c = load_that_starts_at.get(layers[n])
-                if c is not None and c + RAW_BUFS - 1 < len(loads):
-                    load(c + RAW_BUFS - 1)
-                regroup(*layers[n])
-            if 0 <= n - QUANTISE_LAG < len(layers):
-                quantise_and_multiply(*layers[n - QUANTISE_LAG])
-            if 0 <= n - EVACUATE_LAG < len(layers):
-                i, l = layers[n - EVACUATE_LAG]
-                if l == i:
-                    evacuate(i)
-            if 0 <= n - STORE_LAG < len(layers):
-                i, l = layers[n - STORE_LAG]
-                if l == i:
-                    store(i)
+        ctx.enter_context(tc.manual_schedule())
+        for n in range(len(pairs) + STORE_LAG):
+            if n < len(pairs):
+                for layer in pairs[n]:
+                    c = load_that_starts_at.get(layer)
+                    if c is not None and c + RAW_BUFS - 1 < len(loads):
+                        load(c + RAW_BUFS - 1)
+                regroup(n)
+            if 0 <= n - 1 < X_PARTS:
+                turn_x(n - 1)
+            if 0 <= n - QUANTISE_LAG < len(pairs):
+                quantise(n - QUANTISE_LAG)
+            if 0 <= n - MULTIPLY_LAG < X_PARTS:
+                quantise_x(n - MULTIPLY_LAG)
+            if 0 <= n - MULTIPLY_LAG < len(pairs):
+                multiply(n - MULTIPLY_LAG)
+            if 0 <= n - EVACUATE_LAG < len(pairs):
+                for i, l in pairs[n - EVACUATE_LAG]:
+                    if l == i:
+                        evacuate(i)
+            if 0 <= n - STORE_LAG < len(pairs):
+                for i, l in pairs[n - STORE_LAG]:
+                    if l == i:
+                        store(i)

@@ -17,21 +17,21 @@ F = P * PACK
 A = 384
 
 COLUMN_GROUPS = ((0, 256), (256, 384))
-QUANTISE_GROUPS = ((0, 512), (512, 768))
+QUANTISE_GROUPS = {2: ((0, 512), (512, 768)), 1: ((0, 256), (256, 384))}
+
+SINGLE_OUTPUTS = 4
 
 SHARED_VECTOR_COLS = 256
+SINGLE_VECTOR_COLS = 128
+TURNED_COLS = 128
 
-FIRST_LOADS = (1, 1, 2, 2, 2)
 LOAD_LAYERS = 4
+FIRST_LOADS = (1, 1, 2, 2, 2)
+LAST_SHARE = 3
 RAW_BUFS = 9
 X_PARTS = 3
 X_LAYERS = LAYERS // X_PARTS
 X_AFTER = 2
-
-QUANTISE_LAG = 1
-MULTIPLY_LAG = 2
-EVACUATE_LAG = 4
-STORE_LAG = 5
 
 FLOPS = 2 * B * F * A * (LAYERS * (LAYERS + 1) // 2)
 
@@ -57,16 +57,21 @@ def tile_decoder_pa_kernel(
 
         outputs = list(reversed(range(LAYERS)))
         layers = [(i, l) for i in outputs for l in range(i + 1)]
-        pairs = [layers[n : n + 2] for n in range(0, len(layers), 2)]
+        paired = [layer for layer in layers if layer[0] >= SINGLE_OUTPUTS]
+        units = [paired[n : n + 2] for n in range(0, len(paired), 2)]
+        units += [[layer] for layer in layers if layer[0] < SINGLE_OUTPUTS]
+        last = len(units) - 1
 
         loads = []
+        to_come = len(layers)
         for i in outputs:
             l0 = 0
             while l0 <= i:
                 count = FIRST_LOADS[len(loads)] if len(loads) < len(FIRST_LOADS) else LOAD_LAYERS
-                count = min(count, i + 1 - l0)
+                count = min(count, i + 1 - l0, max(1, to_come // LAST_SHARE))
                 loads.append((i, l0, count))
                 l0 += count
+                to_come -= count
         load_that_starts_at = dict(((i, l0), c) for c, (i, l0, count) in enumerate(loads))
         raw_of = {}
 
@@ -93,6 +98,8 @@ def tile_decoder_pa_kernel(
 
         identity = keep.tile([P, P], F32)
         make_identity(nc, identity[:])
+        identity_bf16 = keep.tile([P, P], BF16)
+        make_identity(nc, identity_bf16[:])
         x_words = x_rows[:].rearrange("b l f -> b (l f)").bitcast(F32)
         x_words = x_words.rearrange("b (l p u) -> b l u p", l=LAYERS, u=2)
         x_grouped = keep.tile([P, LAYERS * B * PACK], BF16, align_bytes=64)
@@ -122,33 +129,50 @@ def tile_decoder_pa_kernel(
             )
 
         grouped_of = {}
+        codes_of = {}
         acc_of = {}
-        result_of = {}
 
         def regroup(n):
-            grouped = grouped_pool.tile([P, 2 * A, PACK], BF16, align_bytes=64)
+            grouped = grouped_pool.tile([P, len(units[n]) * A, PACK], BF16, align_bytes=64)
             grouped_of[n] = grouped
-            for y, layer in enumerate(pairs[n]):
+            for y, layer in enumerate(units[n]):
                 raw = raw_of[layer]
-                vector_cols = SHARED_VECTOR_COLS if n in (0, len(pairs) - 1) else (1 - y) * A
+                turned_by_tensor = len(units[n]) == 1 and n < last
+                if turned_by_tensor:
+                    vector_cols = SINGLE_VECTOR_COLS
+                elif n in (0, last):
+                    vector_cols = SHARED_VECTOR_COLS
+                else:
+                    vector_cols = (1 - y) * A
                 if vector_cols > 0:
                     nc.vector.tensor_copy(
                         out=runs_of_four(grouped[:, y * A : y * A + vector_cols, :], "p (c i) t"),
                         in_=runs_of_four(raw[:, :, :vector_cols], "p t (c i)"),
                     )
-                if vector_cols < A:
+                if turned_by_tensor:
+                    turned = turned_pool.tile([P, A - vector_cols, PACK], BF16)
+                    for a0 in range(vector_cols, A, TURNED_COLS):
+                        a1 = a0 + TURNED_COLS
+                        nc.tensor.matmul(
+                            turned[:, a0 - vector_cols : a1 - vector_cols, :].rearrange("p a t -> p (a t)"),
+                            lhsT=identity_bf16[:],
+                            rhs=raw[:, :, a0:a1].rearrange("p t a -> p a t"),
+                            start=True,
+                            stop=True,
+                        )
+                    nc.scalar.copy(out=grouped[:, vector_cols:, :], in_=turned[:])
+                elif vector_cols < A:
                     nc.scalar.copy(
                         out=runs_of_four(grouped[:, y * A + vector_cols : (y + 1) * A, :], "p (c i) t"),
                         in_=runs_of_four(raw[:, :, vector_cols:], "p t (c i)"),
                     )
 
-        codes_of = {}
-
         def quantise(n):
+            columns = len(units[n]) * A
             values = grouped_of[n][:].rearrange("p a t -> p (a t)")
-            codes = codes_pool.tile([P, 2 * A], U32, align_bytes=64)
-            scales = codes_pool.tile([P, 2 * A], U8, align_bytes=64)
-            for first, end in QUANTISE_GROUPS:
+            codes = codes_pool.tile([P, columns], U32, align_bytes=64)
+            scales = codes_pool.tile([P, columns], U8, align_bytes=64)
+            for first, end in QUANTISE_GROUPS[len(units[n])]:
                 nc.vector.quantize_mx(
                     out=codes[:, first:end].bitcast(FP8X4),
                     scales=scales[:, first:end],
@@ -158,7 +182,7 @@ def tile_decoder_pa_kernel(
 
         def multiply(n):
             codes, scales = codes_of[n]
-            for y, (i, l) in enumerate(pairs[n]):
+            for y, (i, l) in enumerate(units[n]):
                 for first, end in COLUMN_GROUPS:
                     if l == 0:
                         acc = acc_pool.tile([B, end - first], F32, tag="acc%d" % first)
@@ -173,36 +197,45 @@ def tile_decoder_pa_kernel(
                         stop=(l == i),
                     )
 
-        def evacuate(i):
-            result = result_pool.tile([B, A], F32)
-            for first, end in COLUMN_GROUPS:
-                nc.scalar.copy(out=result[:, first:end], in_=acc_of[(i, first)][:])
-            result_of[i] = result
+        def evacuate_and_store(n):
+            for i, l in units[n]:
+                if l == i:
+                    result = result_pool.tile([B, A], F32)
+                    for first, end in COLUMN_GROUPS:
+                        if n == last and first > 0:
+                            nc.vector.tensor_copy(out=result[:, first:end], in_=acc_of[(i, first)][:])
+                        else:
+                            nc.scalar.copy(out=result[:, first:end], in_=acc_of[(i, first)][:])
+                    nc.sync.dma_start(out=out[:, i, :], in_=result[:])
 
-        def store(i):
-            nc.sync.dma_start(out=out[:, i, :], in_=result_of[i][:])
+        def quantise_step(n):
+            return n + 1 if n < last - 1 else n
+
+        def multiply_step(n):
+            return n + 2 if n < 2 * X_PARTS else quantise_step(n)
+
+        def evacuate_step(n):
+            if n == last:
+                return n
+            return n + 3 if len(units[n]) == 2 else n + 1
 
         ctx.enter_context(tc.manual_schedule())
-        for n in range(len(pairs) + STORE_LAG):
-            if n < len(pairs):
-                for layer in pairs[n]:
-                    c = load_that_starts_at.get(layer)
-                    if c is not None and c + RAW_BUFS - 1 < len(loads):
-                        load(c + RAW_BUFS - 1)
-                regroup(n)
-            if 0 <= n - 1 < X_PARTS:
-                turn_x(n - 1)
-            if 0 <= n - QUANTISE_LAG < len(pairs):
-                quantise(n - QUANTISE_LAG)
-            if 0 <= n - MULTIPLY_LAG < X_PARTS:
-                quantise_x(n - MULTIPLY_LAG)
-            if 0 <= n - MULTIPLY_LAG < len(pairs):
-                multiply(n - MULTIPLY_LAG)
-            if 0 <= n - EVACUATE_LAG < len(pairs):
-                for i, l in pairs[n - EVACUATE_LAG]:
-                    if l == i:
-                        evacuate(i)
-            if 0 <= n - STORE_LAG < len(pairs):
-                for i, l in pairs[n - STORE_LAG]:
-                    if l == i:
-                        store(i)
+        for step in range(last + 1):
+            for layer in units[step]:
+                c = load_that_starts_at.get(layer)
+                if c is not None and c + RAW_BUFS - 1 < len(loads):
+                    load(c + RAW_BUFS - 1)
+            regroup(step)
+            if 0 <= step - 1 < X_PARTS:
+                turn_x(step - 1)
+            for n in range(step + 1):
+                if quantise_step(n) == step:
+                    quantise(n)
+            if 0 <= step - 2 < X_PARTS:
+                quantise_x(step - 2)
+            for n in range(step + 1):
+                if multiply_step(n) == step:
+                    multiply(n)
+            for n in range(step + 1):
+                if evacuate_step(n) == step:
+                    evacuate_and_store(n)

@@ -22,8 +22,7 @@ QUANTISE_GROUPS = {2: ((0, 512), (512, 768)), 1: ((0, 256), (256, 384))}
 SINGLE_OUTPUTS = 4
 
 SHARED_VECTOR_COLS = 256
-SINGLE_VECTOR_COLS = 128
-TURNED_COLS = 128
+SINGLE_VECTOR_COLS = 192
 
 LOAD_LAYERS = 4
 FIRST_LOADS = (1, 1, 2, 2, 2)
@@ -98,8 +97,6 @@ def tile_decoder_pa_kernel(
 
         identity = keep.tile([P, P], F32)
         make_identity(nc, identity[:])
-        identity_bf16 = keep.tile([P, P], BF16)
-        make_identity(nc, identity_bf16[:])
         x_words = x_rows[:].rearrange("b l f -> b (l f)").bitcast(F32)
         x_words = x_words.rearrange("b (l p u) -> b l u p", l=LAYERS, u=2)
         x_grouped = keep.tile([P, LAYERS * B * PACK], BF16, align_bytes=64)
@@ -137,11 +134,10 @@ def tile_decoder_pa_kernel(
             grouped_of[n] = grouped
             for y, layer in enumerate(units[n]):
                 raw = raw_of[layer]
-                turned_by_tensor = len(units[n]) == 1 and n < last
-                if turned_by_tensor:
-                    vector_cols = SINGLE_VECTOR_COLS
-                elif n in (0, last):
+                if n in (0, last):
                     vector_cols = SHARED_VECTOR_COLS
+                elif len(units[n]) == 1:
+                    vector_cols = SINGLE_VECTOR_COLS
                 else:
                     vector_cols = (1 - y) * A
                 if vector_cols > 0:
@@ -149,19 +145,7 @@ def tile_decoder_pa_kernel(
                         out=runs_of_four(grouped[:, y * A : y * A + vector_cols, :], "p (c i) t"),
                         in_=runs_of_four(raw[:, :, :vector_cols], "p t (c i)"),
                     )
-                if turned_by_tensor:
-                    turned = turned_pool.tile([P, A - vector_cols, PACK], BF16)
-                    for a0 in range(vector_cols, A, TURNED_COLS):
-                        a1 = a0 + TURNED_COLS
-                        nc.tensor.matmul(
-                            turned[:, a0 - vector_cols : a1 - vector_cols, :].rearrange("p a t -> p (a t)"),
-                            lhsT=identity_bf16[:],
-                            rhs=raw[:, :, a0:a1].rearrange("p t a -> p a t"),
-                            start=True,
-                            stop=True,
-                        )
-                    nc.scalar.copy(out=grouped[:, vector_cols:, :], in_=turned[:])
-                elif vector_cols < A:
+                if vector_cols < A:
                     nc.scalar.copy(
                         out=runs_of_four(grouped[:, y * A + vector_cols : (y + 1) * A, :], "p (c i) t"),
                         in_=runs_of_four(raw[:, :, vector_cols:], "p t (c i)"),

@@ -1,3 +1,4 @@
+import math
 from contextlib import ExitStack
 
 import concourse.mybir as mybir
@@ -24,13 +25,13 @@ SINGLE_OUTPUTS = 4
 SHARED_VECTOR_COLS = 256
 SINGLE_VECTOR_COLS = 192
 
-LOAD_LAYERS = 4
-FIRST_LOADS = (1, 1, 2, 2, 2)
+LOAD_LAYERS = 6
+FIRST_LOADS = (2, 2, 4)
 LAST_SHARE = 3
-RAW_BUFS = 9
+RAW_BUFS = 7
 X_PARTS = 3
 X_LAYERS = LAYERS // X_PARTS
-X_AFTER = 2
+X_AFTER = 0
 
 FLOPS = 2 * B * F * A * (LAYERS * (LAYERS + 1) // 2)
 
@@ -66,8 +67,11 @@ def tile_decoder_pa_kernel(
         for i in outputs:
             l0 = 0
             while l0 <= i:
-                count = FIRST_LOADS[len(loads)] if len(loads) < len(FIRST_LOADS) else LOAD_LAYERS
-                count = min(count, i + 1 - l0, max(1, to_come // LAST_SHARE))
+                rest = i + 1 - l0
+                count = math.ceil(rest / math.ceil(rest / LOAD_LAYERS))
+                if len(loads) < len(FIRST_LOADS):
+                    count = FIRST_LOADS[len(loads)]
+                count = min(count, max(1, to_come // LAST_SHARE))
                 loads.append((i, l0, count))
                 l0 += count
                 to_come -= count
@@ -201,7 +205,7 @@ def tile_decoder_pa_kernel(
         def evacuate_step(n):
             if n == last:
                 return n
-            return n + 3 if len(units[n]) == 2 else n + 1
+            return n + 3 if len(units[n]) == 2 else min(n + 2, last)
 
         ctx.enter_context(tc.manual_schedule())
         for step in range(last + 1):

@@ -33,6 +33,8 @@ X_PARTS = 3
 X_LAYERS = LAYERS // X_PARTS
 X_AFTER = 0
 
+STORED_WITH = {4: 11, 1: 3, 0: 0}
+
 FLOPS = 2 * B * F * A * (LAYERS * (LAYERS + 1) // 2)
 
 
@@ -49,9 +51,8 @@ def tile_decoder_pa_kernel(
     with ExitStack() as ctx:
         keep = ctx.enter_context(tc.tile_pool(name="keep", bufs=1))
         raw_pool = ctx.enter_context(tc.tile_pool(name="raw", bufs=RAW_BUFS))
-        grouped_pool = ctx.enter_context(tc.tile_pool(name="grouped", bufs=6))
+        grouped_pool = ctx.enter_context(tc.tile_pool(name="grouped", bufs=5))
         codes_pool = ctx.enter_context(tc.tile_pool(name="codes", bufs=5))
-        result_pool = ctx.enter_context(tc.tile_pool(name="result", bufs=3))
         turned_pool = ctx.enter_context(tc.psum_pool(name="turned", bufs=2))
         acc_pool = ctx.enter_context(tc.psum_pool(name="acc", bufs=3))
 
@@ -132,6 +133,7 @@ def tile_decoder_pa_kernel(
         grouped_of = {}
         codes_of = {}
         acc_of = {}
+        results = keep.tile([B, LAYERS, A], F32)
 
         def regroup(n):
             grouped = grouped_pool.tile([P, len(units[n]) * A, PACK], BF16, align_bytes=64)
@@ -188,13 +190,14 @@ def tile_decoder_pa_kernel(
         def evacuate_and_store(n):
             for i, l in units[n]:
                 if l == i:
-                    result = result_pool.tile([B, A], F32)
                     for first, end in COLUMN_GROUPS:
                         if n == last and first > 0:
-                            nc.vector.tensor_copy(out=result[:, first:end], in_=acc_of[(i, first)][:])
+                            nc.vector.tensor_copy(out=results[:, i, first:end], in_=acc_of[(i, first)][:])
                         else:
-                            nc.scalar.copy(out=result[:, first:end], in_=acc_of[(i, first)][:])
-                    nc.sync.dma_start(out=out[:, i, :], in_=result[:])
+                            nc.scalar.copy(out=results[:, i, first:end], in_=acc_of[(i, first)][:])
+                    if i in STORED_WITH:
+                        stored = slice(i, STORED_WITH[i] + 1)
+                        nc.sync.dma_start(out=out[:, stored, :], in_=results[:, stored, :])
 
         def quantise_step(n):
             return n + 1 if n < last - 1 else n

@@ -20,18 +20,23 @@ A = 384
 COLUMN_GROUPS = ((0, 256), (256, 384))
 QUANTISE_GROUPS = {2: ((0, 512), (512, 768)), 1: ((0, 256), (256, 384))}
 
-SINGLE_OUTPUTS = 4
+SINGLE_OUTPUTS = 3
+
+VECTOR_COLS = 360
+TURNED_EVERY = 5
+TURNED_COLS = 128
+TURN_AHEAD = 2
 
 SHARED_VECTOR_COLS = 256
 SINGLE_VECTOR_COLS = 192
 
-LOAD_LAYERS = 6
-FIRST_LOADS = (2, 2, 4)
+LOAD_LAYERS = 2
+FIRST_LOADS = (1, 1, 1, 1)
 LAST_SHARE = 3
-RAW_BUFS = 7
+RAW_BUFS = 16
 X_PARTS = 3
 X_LAYERS = LAYERS // X_PARTS
-X_AFTER = 0
+X_AFTER = 3
 
 STORED_WITH = {4: 11, 1: 3, 0: 0}
 
@@ -51,7 +56,7 @@ def tile_decoder_pa_kernel(
     with ExitStack() as ctx:
         keep = ctx.enter_context(tc.tile_pool(name="keep", bufs=1))
         raw_pool = ctx.enter_context(tc.tile_pool(name="raw", bufs=RAW_BUFS))
-        grouped_pool = ctx.enter_context(tc.tile_pool(name="grouped", bufs=5))
+        grouped_pool = ctx.enter_context(tc.tile_pool(name="grouped", bufs=6))
         codes_pool = ctx.enter_context(tc.tile_pool(name="codes", bufs=5))
         turned_pool = ctx.enter_context(tc.psum_pool(name="turned", bufs=2))
         acc_pool = ctx.enter_context(tc.psum_pool(name="acc", bufs=3))
@@ -102,6 +107,8 @@ def tile_decoder_pa_kernel(
 
         identity = keep.tile([P, P], F32)
         make_identity(nc, identity[:])
+        identity_bf16 = keep.tile([P, P], BF16)
+        make_identity(nc, identity_bf16[:])
         x_words = x_rows[:].rearrange("b l f -> b (l f)").bitcast(F32)
         x_words = x_words.rearrange("b (l p u) -> b l u p", l=LAYERS, u=2)
         x_grouped = keep.tile([P, LAYERS * B * PACK], BF16, align_bytes=64)
@@ -135,6 +142,26 @@ def tile_decoder_pa_kernel(
         acc_of = {}
         results = keep.tile([B, LAYERS, A], F32)
 
+        turned_of = {}
+
+        def is_turned(n):
+            return n > 0 and n % TURNED_EVERY == 0 and n < len(units) and len(units[n]) == 2
+
+        def turn(n):
+            raw = raw_of[units[n][1]]
+            turned_of[n] = []
+            for first, end in COLUMN_GROUPS:
+                turned = turned_pool.tile([P, end - first, PACK], BF16)
+                for a0 in range(first, end, TURNED_COLS):
+                    nc.tensor.matmul(
+                        turned[:, a0 - first : a0 - first + TURNED_COLS, :].rearrange("p a t -> p (a t)"),
+                        lhsT=identity_bf16[:],
+                        rhs=raw[:, :, a0 : a0 + TURNED_COLS].rearrange("p t a -> p a t"),
+                        start=True,
+                        stop=True,
+                    )
+                turned_of[n].append(turned)
+
         def regroup(n):
             grouped = grouped_pool.tile([P, len(units[n]) * A, PACK], BF16, align_bytes=64)
             grouped_of[n] = grouped
@@ -145,13 +172,16 @@ def tile_decoder_pa_kernel(
                 elif len(units[n]) == 1:
                     vector_cols = SINGLE_VECTOR_COLS
                 else:
-                    vector_cols = (1 - y) * A
+                    vector_cols = (1 - y) * VECTOR_COLS
                 if vector_cols > 0:
                     nc.vector.tensor_copy(
                         out=runs_of_four(grouped[:, y * A : y * A + vector_cols, :], "p (c i) t"),
                         in_=runs_of_four(raw[:, :, :vector_cols], "p t (c i)"),
                     )
-                if vector_cols < A:
+                if y == 1 and is_turned(n):
+                    for (first, end), turned in zip(COLUMN_GROUPS, turned_of[n]):
+                        nc.scalar.copy(out=grouped[:, A + first : A + end, :], in_=turned[:])
+                elif vector_cols < A:
                     nc.scalar.copy(
                         out=runs_of_four(grouped[:, y * A + vector_cols : (y + 1) * A, :], "p (c i) t"),
                         in_=runs_of_four(raw[:, :, vector_cols:], "p t (c i)"),
@@ -219,6 +249,8 @@ def tile_decoder_pa_kernel(
             regroup(step)
             if 0 <= step - 1 < X_PARTS:
                 turn_x(step - 1)
+            if is_turned(step + TURN_AHEAD):
+                turn(step + TURN_AHEAD)
             for n in range(step + 1):
                 if quantise_step(n) == step:
                     quantise(n)

import math
from contextlib import ExitStack

import concourse.mybir as mybir
from concourse.masks import make_identity

BF16 = mybir.dt.bfloat16
F32 = mybir.dt.float32
U32 = mybir.dt.uint32
U8 = mybir.dt.uint8
FP8X4 = mybir.dt.float8_e4m3fn_x4

P = 128
PACK = 4
B = 128
LAYERS = 12
F = P * PACK
A = 384

COLUMN_GROUPS = ((0, 256), (256, 384))
QUANTISE_GROUPS = {2: ((0, 512), (512, 768)), 1: ((0, 256), (256, 384))}

SINGLE_OUTPUTS = 3

VECTOR_COLS = 360
TURNED_EVERY = 5
TURNED_COLS = 128
TURN_AHEAD = 2

SHARED_VECTOR_COLS = 256
SINGLE_VECTOR_COLS = 192

LOAD_LAYERS = 2
FIRST_LOADS = (1, 1, 1, 1)
LAST_SHARE = 3
RAW_BUFS = 16
X_PARTS = 3
X_LAYERS = LAYERS // X_PARTS
X_AFTER = 3

STORED_WITH = {4: 11, 1: 3, 0: 0}

FLOPS = 2 * B * F * A * (LAYERS * (LAYERS + 1) // 2)


def runs_of_four(view, order):
    return view.rearrange(order + " -> p c t i", i=4)


def tile_decoder_pa_kernel(
    tc, x, W_0, W_1, W_2, W_3, W_4, W_5, W_6, W_7, W_8, W_9, W_10, W_11, out
):
    nc = tc.nc
    weights = [W_0, W_1, W_2, W_3, W_4, W_5, W_6, W_7, W_8, W_9, W_10, W_11]

    with ExitStack() as ctx:
        keep = ctx.enter_context(tc.tile_pool(name="keep", bufs=1))
        raw_pool = ctx.enter_context(tc.tile_pool(name="raw", bufs=RAW_BUFS))
        grouped_pool = ctx.enter_context(tc.tile_pool(name="grouped", bufs=6))
        codes_pool = ctx.enter_context(tc.tile_pool(name="codes", bufs=5))
        turned_pool = ctx.enter_context(tc.psum_pool(name="turned", bufs=2))
        acc_pool = ctx.enter_context(tc.psum_pool(name="acc", bufs=3))

        outputs = list(reversed(range(LAYERS)))
        layers = [(i, l) for i in outputs for l in range(i + 1)]
        paired = [layer for layer in layers if layer[0] >= SINGLE_OUTPUTS]
        units = [paired[n : n + 2] for n in range(0, len(paired), 2)]
        units += [[layer] for layer in layers if layer[0] < SINGLE_OUTPUTS]
        last = len(units) - 1

        loads = []
        to_come = len(layers)
        for i in outputs:
            l0 = 0
            while l0 <= i:
                rest = i + 1 - l0
                count = math.ceil(rest / math.ceil(rest / LOAD_LAYERS))
                if len(loads) < len(FIRST_LOADS):
                    count = FIRST_LOADS[len(loads)]
                count = min(count, max(1, to_come // LAST_SHARE))
                loads.append((i, l0, count))
                l0 += count
                to_come -= count
        load_that_starts_at = dict(((i, l0), c) for c, (i, l0, count) in enumerate(loads))
        raw_of = {}

        def load(c):
            i, l0, count = loads[c]
            raw = raw_pool.tile([P, LOAD_LAYERS, PACK, A], BF16)
            nc.sync.dma_start(
                out=raw[:, :count],
                in_=weights[i][l0 : l0 + count].rearrange("l (p t) a -> p l t a", t=PACK),
            )
            for y in range(count):
                raw_of[(i, l0 + y)] = raw[:, y]

        x_rows = keep.tile([B, LAYERS, F], BF16)

        def load_x(part):
            part_layers = slice(part * X_LAYERS, (part + 1) * X_LAYERS)
            nc.sync.dma_start(out=x_rows[:, part_layers, :], in_=x[:, part_layers, :])

        for c in range(RAW_BUFS - 1):
            load(c)
            if 0 <= c - X_AFTER < X_PARTS:
                load_x(c - X_AFTER)

        identity = keep.tile([P, P], F32)
        make_identity(nc, identity[:])
        identity_bf16 = keep.tile([P, P], BF16)
        make_identity(nc, identity_bf16[:])
        x_words = x_rows[:].rearrange("b l f -> b (l f)").bitcast(F32)
        x_words = x_words.rearrange("b (l p u) -> b l u p", l=LAYERS, u=2)
        x_grouped = keep.tile([P, LAYERS * B * PACK], BF16, align_bytes=64)
        x_grouped_words = x_grouped[:].bitcast(F32).rearrange("p (l b u) -> p l b u", l=LAYERS, u=2)
        x_codes = keep.tile([P, LAYERS * B], U32, align_bytes=64)
        x_scales = keep.tile([P, LAYERS * B], U8, align_bytes=64)

        def turn_x(part):
            first = part * X_LAYERS
            for l0 in range(first, first + X_LAYERS, 2):
                turned = turned_pool.tile([P, 2, 2, B], F32)
                for y in range(2):
                    for u in range(2):
                        nc.tensor.transpose(turned[:, y, u, :], x_words[:, l0 + y, u, :], identity[:])
                nc.scalar.copy(
                    out=x_grouped_words[:, l0 : l0 + 2],
                    in_=turned[:].rearrange("p y u b -> p y b u"),
                )

        def quantise_x(part):
            first = part * X_LAYERS
            columns = slice(first * B, (first + X_LAYERS) * B)
            nc.vector.quantize_mx(
                out=x_codes[:, columns].bitcast(FP8X4),
                scales=x_scales[:, columns],
                in_=x_grouped[:, first * B * PACK : (first + X_LAYERS) * B * PACK],
            )

        grouped_of = {}
        codes_of = {}
        acc_of = {}
        results = keep.tile([B, LAYERS, A], F32)

        turned_of = {}

        def is_turned(n):
            return n > 0 and n % TURNED_EVERY == 0 and n < len(units) and len(units[n]) == 2

        def turn(n):
            raw = raw_of[units[n][1]]
            turned_of[n] = []
            for first, end in COLUMN_GROUPS:
                turned = turned_pool.tile([P, end - first, PACK], BF16)
                for a0 in range(first, end, TURNED_COLS):
                    nc.tensor.matmul(
                        turned[:, a0 - first : a0 - first + TURNED_COLS, :].rearrange("p a t -> p (a t)"),
                        lhsT=identity_bf16[:],
                        rhs=raw[:, :, a0 : a0 + TURNED_COLS].rearrange("p t a -> p a t"),
                        start=True,
                        stop=True,
                    )
                turned_of[n].append(turned)

        def regroup(n):
            grouped = grouped_pool.tile([P, len(units[n]) * A, PACK], BF16, align_bytes=64)
            grouped_of[n] = grouped
            for y, layer in enumerate(units[n]):
                raw = raw_of[layer]
                if n in (0, last):
                    vector_cols = SHARED_VECTOR_COLS
                elif len(units[n]) == 1:
                    vector_cols = SINGLE_VECTOR_COLS
                else:
                    vector_cols = (1 - y) * VECTOR_COLS
                if vector_cols > 0:
                    nc.vector.tensor_copy(
                        out=runs_of_four(grouped[:, y * A : y * A + vector_cols, :], "p (c i) t"),
                        in_=runs_of_four(raw[:, :, :vector_cols], "p t (c i)"),
                    )
                if y == 1 and is_turned(n):
                    for (first, end), turned in zip(COLUMN_GROUPS, turned_of[n]):
                        nc.scalar.copy(out=grouped[:, A + first : A + end, :], in_=turned[:])
                elif vector_cols < A:
                    nc.scalar.copy(
                        out=runs_of_four(grouped[:, y * A + vector_cols : (y + 1) * A, :], "p (c i) t"),
                        in_=runs_of_four(raw[:, :, vector_cols:], "p t (c i)"),
                    )

        def quantise(n):
            columns = len(units[n]) * A
            values = grouped_of[n][:].rearrange("p a t -> p (a t)")
            codes = codes_pool.tile([P, columns], U32, align_bytes=64)
            scales = codes_pool.tile([P, columns], U8, align_bytes=64)
            for first, end in QUANTISE_GROUPS[len(units[n])]:
                nc.vector.quantize_mx(
                    out=codes[:, first:end].bitcast(FP8X4),
                    scales=scales[:, first:end],
                    in_=values[:, first * PACK : end * PACK],
                )
            codes_of[n] = (codes, scales)

        def multiply(n):
            codes, scales = codes_of[n]
            for y, (i, l) in enumerate(units[n]):
                for first, end in COLUMN_GROUPS:
                    if l == 0:
                        acc = acc_pool.tile([B, end - first], F32, tag="acc%d" % first)
                        acc_of[(i, first)] = acc
                    nc.tensor.matmul_mx(
                        out=acc_of[(i, first)][:],
                        lhsT=x_codes[:, l * B : (l + 1) * B].bitcast(FP8X4),
                        lhsT_scale=x_scales[:, l * B : (l + 1) * B],
                        rhs=codes[:, y * A + first : y * A + end].bitcast(FP8X4),
                        rhs_scale=scales[:, y * A + first : y * A + end],
                        start=(l == 0),
                        stop=(l == i),
                    )

        def evacuate_and_store(n):
            for i, l in units[n]:
                if l == i:
                    for first, end in COLUMN_GROUPS:
                        if n == last and first > 0:
                            nc.vector.tensor_copy(out=results[:, i, first:end], in_=acc_of[(i, first)][:])
                        else:
                            nc.scalar.copy(out=results[:, i, first:end], in_=acc_of[(i, first)][:])
                    if i in STORED_WITH:
                        stored = slice(i, STORED_WITH[i] + 1)
                        nc.sync.dma_start(out=out[:, stored, :], in_=results[:, stored, :])

        def quantise_step(n):
            return n + 1 if n < last - 1 else n

        def multiply_step(n):
            return n + 2 if n < 2 * X_PARTS else quantise_step(n)

        def evacuate_step(n):
            if n == last:
                return n
            return n + 3 if len(units[n]) == 2 else min(n + 2, last)

        ctx.enter_context(tc.manual_schedule())
        for step in range(last + 1):
            for layer in units[step]:
                c = load_that_starts_at.get(layer)
                if c is not None and c + RAW_BUFS - 1 < len(loads):
                    load(c + RAW_BUFS - 1)
            regroup(step)
            if 0 <= step - 1 < X_PARTS:
                turn_x(step - 1)
            if is_turned(step + TURN_AHEAD):
                turn(step + TURN_AHEAD)
            for n in range(step + 1):
                if quantise_step(n) == step:
                    quantise(n)
            if 0 <= step - 2 < X_PARTS:
                quantise_x(step - 2)
            for n in range(step + 1):
                if multiply_step(n) == step:
                    multiply(n)
            for n in range(step + 1):
                if evacuate_step(n) == step:
                    evacuate_and_store(n)
